import numpy as np
import ml_dtypes


def mxq(x, axis, fmt="e4m3"):
    dtype, down = {"e4m3": (ml_dtypes.float8_e4m3fn, 7), "e5m2": (ml_dtypes.float8_e5m2, 14)}[fmt]
    v = np.moveaxis(np.asarray(x, np.float32).astype(ml_dtypes.bfloat16).astype(np.float64), axis, -1)
    blocks = v.reshape(v.shape[:-1] + (-1, 32))
    amax = np.abs(blocks).max(-1, keepdims=True)
    byte = np.maximum(np.where(amax > 0, np.frexp(amax)[1] - 1 + 127, 0) - down, 1)
    scale = np.exp2(byte - 127.0)
    codes = (blocks / scale).astype(np.float32).astype(dtype).astype(np.float64)
    return np.moveaxis((codes * scale).reshape(v.shape), -1, axis)


WIDE = False


def mx_kscale(k):
    if not WIDE:
        return np.ones(k)
    levels = np.array([10, -10, 5, -5, 0])
    if k % 512:
        return np.exp2(np.random.permutation(np.resize(levels, k // 32))).repeat(32)
    a = np.empty((k // 512, 16))
    for p in range(k // 512):
        a[p, :8] = np.random.permutation(np.resize(levels, 8))
        for g in range(8):
            far = levels[np.abs(levels - a[p, g]) >= 10]
            a[p, g + 8] = far[np.random.randint(len(far))]
    return np.exp2(a.ravel()).repeat(32)


BF16 = ml_dtypes.bfloat16


def bf(x):
    return np.asarray(x, np.float32).astype(BF16)


def f64(x):
    return np.asarray(x).astype(np.float64)


B, I, H, ORDER = 256, 8192, 512, 3
OH = ORDER * H


def sigmoid(v):
    return 1.0 / (1.0 + np.exp(-v))


def setup_inputs():
    s, t = mx_kscale(I), mx_kscale(OH)
    return {"x": bf(np.random.standard_normal((B, I)) * s),
            "me_output": bf(np.random.standard_normal((B, OH)) * t),
            "W_memi": bf(np.random.standard_normal((I, OH)) * 0.7 / np.sqrt(I) / s[:, None]),
            "W_memh": bf(np.random.standard_normal((OH, OH)) * 0.7 / np.sqrt(OH) / t[:, None]),
            "W_memt": bf(np.random.standard_normal((OH, H)) * 1.0 / np.sqrt(OH) / t[:, None]),
            "mem_bias": bf(np.random.standard_normal(OH) * 0.3)}


def reference(x, me_output, W_memi, W_memh, W_memt, mem_bias):
    me = f64(me_output)
    mg = ((mxq(f64(x), 1, "e4m3") @ mxq(f64(W_memi), 0, "e4m3"))
          + (mxq(me, 1, "e4m3") @ mxq(f64(W_memh), 0, "e4m3"))
          + f64(mem_bias))
    gated = sigmoid(mg) * me
    return mxq(gated, 1, "e4m3") @ mxq(f64(W_memt), 0, "e4m3")

@@ -1,0 +1,285 @@
+import concourse.mybir as mybir
+from concourse.masks import make_identity
+
+F32 = mybir.dt.float32
+BF16 = mybir.dt.bfloat16
+U32 = mybir.dt.uint32
+U8 = mybir.dt.uint8
+FP8X4 = mybir.dt.float8_e4m3fn_x4
+ADD = mybir.AluOpType.add
+MULT = mybir.AluOpType.mult
+SIGMOID = mybir.ActivationFunctionType.Sigmoid
+
+B, I, OH, H = 256, 8192, 1536, 512
+FLOPS = 2 * B * (I * OH + OH * OH + OH * H)
+
+P = 128
+PACK = 4
+K_PASS = P * PACK
+N_BLOCK = 512
+B_TILES = B // P
+
+X_PASSES = I // K_PASS
+ME_PASSES = OH // K_PASS
+PASSES = X_PASSES + ME_PASSES
+COL_BLOCKS = OH // N_BLOCK
+
+BLOCKS_PER_RAW = 3
+RAW_TILES = X_PASSES + COL_BLOCKS + 1
+BLOCKS = RAW_TILES * BLOCKS_PER_RAW
+FIRST_MEMORY_BLOCK = X_PASSES * BLOCKS_PER_RAW
+
+SLAB_PASSES = 4
+X_SLABS = X_PASSES // SLAB_PASSES
+LOAD_AHEAD = 5
+TURN_LEAD = 4
+COLLECT_LEAD = 2
+SLAB_LEAD = 3
+LAG = 2
+
+
+def tile_lstmcell_pa_k_kernel(tc, x, me_output, W_memi, W_memh, W_memt, mem_bias, out):
+    nc = tc.nc
+    with (
+        tc.tile_pool(name="const", bufs=1) as const,
+        tc.tile_pool(name="slabs", bufs=3) as slabs,
+        tc.tile_pool(name="raws", bufs=LOAD_AHEAD + 1) as raws,
+        tc.tile_pool(name="stream", bufs=6) as stream,
+        tc.tile_pool(name="gate", bufs=4) as gate_pool,
+        tc.psum_pool(name="sums", bufs=B_TILES * COL_BLOCKS) as sums,
+        tc.psum_pool(name="turn", bufs=2) as turn,
+        tc.manual_schedule(),
+    ):
+        ident_f32 = const.tile([P, P], F32)
+        make_identity(nc, ident_f32[:])
+
+        warm = const.tile([P, 1], F32)
+        nc.vector.memset(warm[:], 0.0)
+        nc.scalar.activation(out=warm[:], in_=warm[:], func=SIGMOID)
+
+        bias_row = const.tile([1, OH], BF16)
+        nc.sync.dma_start(out=bias_row[:], in_=mem_bias.rearrange("(o n) -> o n", o=1))
+        ones = const.tile([P, P], BF16)
+        nc.vector.memset(ones[:], 1.0)
+        bias_rows = const.tile([P, OH], BF16)
+        nc.vector.memset(bias_rows[:], 0.0)
+        nc.vector.tensor_copy(out=bias_rows[0:1, :], in_=bias_row[:])
+        bias_all = const.tile([P, OH], BF16)
+        for cb in range(COL_BLOCKS):
+            cols = slice(cb * N_BLOCK, (cb + 1) * N_BLOCK)
+            spread = turn.tile([P, N_BLOCK], F32, tag="turn", name="spread")
+            nc.tensor.matmul(out=spread[:], lhsT=ones[:], rhs=bias_rows[:, cols], start=True, stop=True)
+            nc.vector.tensor_copy(out=bias_all[:, cols], in_=spread[:])
+
+        act_codes = const.tile([P, PASSES, B], U32, align_bytes=64)
+        act_scales = const.tile([P, PASSES, B], U8, align_bytes=64)
+        gated_codes = const.tile([P, ME_PASSES, B], U32, align_bytes=64)
+        gated_scales = const.tile([P, ME_PASSES, B], U8, align_bytes=64)
+        read_codes = const.tile([P, ME_PASSES, H], U32, align_bytes=64)
+        read_scales = const.tile([P, ME_PASSES, H], U8, align_bytes=64)
+        me_rows = [const.tile([P, OH], BF16, name="me_rows%d" % bt) for bt in range(B_TILES)]
+        x_slabs = []
+        raw_tiles = []
+        grouped_tiles = []
+        turned = {}
+        act_grouped = {}
+        mg = [
+            [sums.tile([P, N_BLOCK], F32, tag="sum", name="mg%d_%d" % (bt, cb)) for cb in range(COL_BLOCKS)]
+            for bt in range(B_TILES)
+        ]
+
+        def load_activations(s):
+            for bt in range(B_TILES):
+                rows = slice(bt * P, (bt + 1) * P)
+                if s < X_SLABS:
+                    if bt == 0:
+                        x_slabs.append([])
+                    slab = slabs.tile([P, SLAB_PASSES * K_PASS], BF16, tag="slab%d" % bt, name="slab%d" % bt)
+                    width = SLAB_PASSES * K_PASS
+                    nc.sync.dma_start(out=slab[:], in_=x[rows, s * width : (s + 1) * width])
+                    x_slabs[s].append(slab)
+                else:
+                    nc.sync.dma_start(out=me_rows[bt][:], in_=me_output[rows, :])
+
+        def load_raw(r):
+            if r + SLAB_LEAD < PASSES and (r + SLAB_LEAD) % SLAB_PASSES == 0:
+                load_activations((r + SLAB_LEAD) // SLAB_PASSES)
+            raw = raws.tile([P, BLOCKS_PER_RAW * PACK * N_BLOCK], BF16, tag="raw", name="raw")
+            if r < X_PASSES:
+                rows_of_pass = W_memi[r * K_PASS : (r + 1) * K_PASS, :].rearrange("(q t) c -> q t c", t=PACK)
+                pieces = BLOCKS_PER_RAW if r == 0 else 1
+                width = OH // pieces
+                for piece in range(pieces):
+                    cols = slice(piece * width, (piece + 1) * width)
+                    nc.sync.dma_start(
+                        out=raw[:].rearrange("q (t c) -> q t c", t=PACK)[:, :, cols], in_=rows_of_pass[:, :, cols]
+                    )
+            elif r < X_PASSES + COL_BLOCKS:
+                cb = r - X_PASSES
+                for g in range(ME_PASSES):
+                    nc.sync.dma_start(
+                        out=raw[:].rearrange("q (g t c) -> q g t c", t=PACK, c=N_BLOCK)[:, g, :, :],
+                        in_=W_memh[g * K_PASS : (g + 1) * K_PASS, cb * N_BLOCK : (cb + 1) * N_BLOCK].rearrange(
+                            "(q t) c -> q t c", t=PACK
+                        ),
+                    )
+            else:
+                for g in range(ME_PASSES):
+                    nc.sync.dma_start(
+                        out=raw[:].rearrange("p (g t c) -> p g t c", t=PACK, c=N_BLOCK)[:, g, :, :],
+                        in_=W_memt[g * K_PASS : (g + 1) * K_PASS, :].rearrange("(p t) c -> p t c", t=PACK),
+                    )
+            raw_tiles.append(raw)
+
+        def block_source(r, i):
+            if r < X_PASSES:
+                return raw_tiles[r][:].rearrange("q (t c) -> q t c", t=PACK)[:, :, i * N_BLOCK : (i + 1) * N_BLOCK]
+            return raw_tiles[r][:].rearrange("p (g t c) -> p g t c", t=PACK, c=N_BLOCK)[:, i, :, :]
+
+        def turn_activations(g):
+            if g < X_PASSES:
+                row_tiles, local = x_slabs[g // SLAB_PASSES], g % SLAB_PASSES
+            else:
+                row_tiles, local = me_rows, g - X_PASSES
+            words = turn.tile([P, B_TILES, 2, P], F32, tag="turn", name="words")
+            for bt in range(B_TILES):
+                as_words = row_tiles[bt][:].bitcast(F32).rearrange("b (q u) -> b q u", u=2)
+                for u in range(2):
+                    nc.tensor.transpose(words[:, bt, u, :], as_words[:, local * P : (local + 1) * P, u], ident_f32[:])
+            turned[g] = words
+
+        def collect_activations(g):
+            grouped = stream.tile([P, B_TILES, P, PACK], BF16, tag="act_grouped", name="act_grouped", bufs=3, align_bytes=64)
+            nc.scalar.copy(out=grouped[:].bitcast(F32), in_=turned[g][:].rearrange("q a u b -> q a b u"))
+            act_grouped[g] = grouped
+
+        def quantise_activations(g):
+            nc.vector.quantize_mx(
+                out=act_codes[:, g, :].bitcast(FP8X4),
+                scales=act_scales[:, g, :],
+                in_=act_grouped[g][:].rearrange("p a b t -> p (a b t)"),
+            )
+
+        def regroup(j):
+            source = block_source(j // BLOCKS_PER_RAW, j % BLOCKS_PER_RAW)
+            grouped = stream.tile([P, N_BLOCK, PACK], BF16, tag="grouped", name="grouped", bufs=8, align_bytes=64)
+            dst = grouped[:].rearrange("p (c i) t -> p c t i", i=4)
+            src = source.rearrange("p t (c i) -> p c t i", i=4)
+            if j % 2 == 0:
+                nc.vector.tensor_copy(out=dst, in_=src)
+            else:
+                nc.scalar.copy(out=dst, in_=src)
+            grouped_tiles.append(grouped)
+
+        def multiply(sum_tiles, codes_of_pass, scales_of_pass, codes, scales, start, stop):
+            for bt in range(B_TILES):
+                rows = slice(bt * P, (bt + 1) * P)
+                nc.tensor.matmul_mx(
+                    out=sum_tiles[bt][:],
+                    lhsT=codes_of_pass[:, rows].bitcast(FP8X4),
+                    lhsT_scale=scales_of_pass[:, rows],
+                    rhs=codes.bitcast(FP8X4),
+                    rhs_scale=scales,
+                    start=start,
+                    stop=stop,
+                )
+
+        def finish(j):
+            r, i = divmod(j, BLOCKS_PER_RAW)
+            if r < X_PASSES + COL_BLOCKS:
+                codes = stream.tile([P, N_BLOCK], U32, tag="codes", name="codes", align_bytes=64)[:]
+                scales = stream.tile([P, N_BLOCK], U8, tag="scales", name="scales", align_bytes=64)[:]
+            else:
+                codes = read_codes[:, i, :]
+                scales = read_scales[:, i, :]
+            nc.vector.quantize_mx(
+                out=codes.bitcast(FP8X4), scales=scales, in_=grouped_tiles[j][:].rearrange("p c t -> p (c t)")
+            )
+            if r < X_PASSES:
+                column = [mg[bt][i] for bt in range(B_TILES)]
+                multiply(column, act_codes[:, r, :], act_scales[:, r, :], codes, scales, r == 0, False)
+            elif r < X_PASSES + COL_BLOCKS:
+                cb = r - X_PASSES
+                g = X_PASSES + i
+                column = [mg[bt][cb] for bt in range(B_TILES)]
+                multiply(column, act_codes[:, g, :], act_scales[:, g, :], codes, scales, False, i == ME_PASSES - 1)
+
+        z_tiles = {}
+        gated_planes = {}
+        gated_grouped = {}
+
+        def add_bias(cb):
+            cols = slice(cb * N_BLOCK, (cb + 1) * N_BLOCK)
+            for bt in range(B_TILES):
+                z = gate_pool.tile([P, N_BLOCK], F32, tag="z", name="z")
+                nc.vector.tensor_tensor(out=z[:], in0=mg[bt][cb][:], in1=bias_all[:, cols], op=ADD)
+                z_tiles[(cb, bt)] = z
+
+        def squash(cb):
+            for bt in range(B_TILES):
+                z = z_tiles[(cb, bt)]
+                nc.scalar.activation(out=z[:], in_=z[:], func=SIGMOID)
+
+        def mask_and_turn(cb):
+            cols = slice(cb * N_BLOCK, (cb + 1) * N_BLOCK)
+            for bt in range(B_TILES):
+                gated = gate_pool.tile([P, N_BLOCK], BF16, tag="gated", name="gated")
+                nc.vector.tensor_tensor(out=gated[:], in0=z_tiles[(cb, bt)][:], in1=me_rows[bt][:, cols], op=MULT)
+                words = turn.tile([P, 2, P], F32, tag="turn", name="gated_words")
+                as_words = gated[:].bitcast(F32).rearrange("b (q u) -> b q u", u=2)
+                for u in range(2):
+                    nc.tensor.transpose(words[:, u, :], as_words[:, :, u], ident_f32[:])
+                gated_planes[(cb, bt)] = words
+
+        def collect(cb):
+            grouped = gate_pool.tile([P, B_TILES, P, PACK], BF16, tag="gated_grouped", name="gated_grouped", bufs=2, align_bytes=64)
+            for bt in range(B_TILES):
+                nc.scalar.copy(
+                    out=grouped[:].bitcast(F32)[:, bt, :, :], in_=gated_planes[(cb, bt)][:].rearrange("q u b -> q b u")
+                )
+            gated_grouped[cb] = grouped
+
+        def quantise_gated(cb):
+            nc.vector.quantize_mx(
+                out=gated_codes[:, cb, :].bitcast(FP8X4),
+                scales=gated_scales[:, cb, :],
+                in_=gated_grouped[cb][:].rearrange("p a b t -> p (a b t)"),
+            )
+
+        gate_stages = (add_bias, squash, mask_and_turn, collect, quantise_gated)
+
+        load_activations(0)
+        for r in range(LOAD_AHEAD):
+            load_raw(r)
+        for step in range(-TURN_LEAD * BLOCKS_PER_RAW, BLOCKS + LAG + len(gate_stages)):
+            r, i = divmod(step, BLOCKS_PER_RAW)
+            if i == 0 and 0 <= r + COLLECT_LEAD < PASSES:
+                collect_activations(r + COLLECT_LEAD)
+            if i == 1 and 0 <= r + TURN_LEAD < PASSES:
+                turn_activations(r + TURN_LEAD)
+            if 0 <= step < BLOCKS:
+                if i == 0 and r + LOAD_AHEAD < RAW_TILES:
+                    load_raw(r + LOAD_AHEAD)
+                regroup(step)
+            if i == 2 and 0 <= r + COLLECT_LEAD < PASSES:
+                quantise_activations(r + COLLECT_LEAD)
+            if LAG <= step < BLOCKS + LAG:
+                finish(step - LAG)
+            for n in range(len(gate_stages)):
+                cb, i_done = divmod(step - LAG - n - 1 - FIRST_MEMORY_BLOCK, BLOCKS_PER_RAW)
+                if 0 <= cb < COL_BLOCKS and i_done == BLOCKS_PER_RAW - 1:
+                    gate_stages[n](cb)
+
+        out_sums = [sums.tile([P, H], F32, tag="sum", name="out_sum%d" % bt) for bt in range(B_TILES)]
+        for g in range(ME_PASSES):
+            multiply(
+                out_sums, gated_codes[:, g, :], gated_scales[:, g, :], read_codes[:, g, :], read_scales[:, g, :],
+                g == 0, g == ME_PASSES - 1,
+            )
+        for bt in range(B_TILES):
+            result = gate_pool.tile([P, H], F32, tag="result", name="result", bufs=2)
+            if bt == 0:
+                nc.scalar.copy(out=result[:], in_=out_sums[bt][:])
+            else:
+                nc.vector.tensor_copy(out=result[:], in_=out_sums[bt][:])
+            nc.sync.dma_start(out=out[bt * P : (bt + 1) * P, :], in_=result[:])

@@ -27,15 +27,20 @@ COL_BLOCKS = OH // N_BLOCK
 BLOCKS_PER_RAW = 3
 RAW_TILES = X_PASSES + COL_BLOCKS + 1
 BLOCKS = RAW_TILES * BLOCKS_PER_RAW
-FIRST_MEMORY_BLOCK = X_PASSES * BLOCKS_PER_RAW
 
 SLAB_PASSES = 4
 X_SLABS = X_PASSES // SLAB_PASSES
+EARLY_TILES = 2
 LOAD_AHEAD = 5
-TURN_LEAD = 4
-COLLECT_LEAD = 2
+TURN_LEAD = 2
 SLAB_LEAD = 3
+CYCLE = 5
+HALF = N_BLOCK // 2
+SPREAD_LEAD = 1
+SPREAD_LAG = 3
 LAG = 2
+PRODUCT_LAG = 3
+LAST_BLOCKS = 12
 
 
 def tile_lstmcell_pa_k_kernel(tc, x, me_output, W_memi, W_memh, W_memt, mem_bias, out):
@@ -44,14 +49,17 @@ def tile_lstmcell_pa_k_kernel(tc, x, me_output, W_memi, W_memh, W_memt, mem_bias
         tc.tile_pool(name="const", bufs=1) as const,
         tc.tile_pool(name="slabs", bufs=3) as slabs,
         tc.tile_pool(name="raws", bufs=LOAD_AHEAD + 1) as raws,
-        tc.tile_pool(name="stream", bufs=6) as stream,
+        tc.tile_pool(name="stream", bufs=8) as stream,
         tc.tile_pool(name="gate", bufs=4) as gate_pool,
         tc.psum_pool(name="sums", bufs=B_TILES * COL_BLOCKS) as sums,
-        tc.psum_pool(name="turn", bufs=2) as turn,
+        tc.psum_pool(name="turn", bufs=1) as turn,
+        tc.psum_pool(name="spread", bufs=1) as spread_pool,
         tc.manual_schedule(),
     ):
         ident_f32 = const.tile([P, P], F32)
         make_identity(nc, ident_f32[:])
+        ident_bf16 = const.tile([P, P], BF16)
+        make_identity(nc, ident_bf16[:])
 
         warm = const.tile([P, 1], F32)
         nc.vector.memset(warm[:], 0.0)
@@ -62,14 +70,14 @@ def tile_lstmcell_pa_k_kernel(tc, x, me_output, W_memi, W_memh, W_memt, mem_bias
         ones = const.tile([P, P], BF16)
         nc.vector.memset(ones[:], 1.0)
         bias_rows = const.tile([P, OH], BF16)
-        nc.vector.memset(bias_rows[:], 0.0)
+        nc.gpsimd.memset(bias_rows[:].bitcast(F32), 0.0)
         nc.vector.tensor_copy(out=bias_rows[0:1, :], in_=bias_row[:])
         bias_all = const.tile([P, OH], BF16)
         for cb in range(COL_BLOCKS):
             cols = slice(cb * N_BLOCK, (cb + 1) * N_BLOCK)
-            spread = turn.tile([P, N_BLOCK], F32, tag="turn", name="spread")
-            nc.tensor.matmul(out=spread[:], lhsT=ones[:], rhs=bias_rows[:, cols], start=True, stop=True)
-            nc.vector.tensor_copy(out=bias_all[:, cols], in_=spread[:])
+            bias_sum = sums.tile([P, N_BLOCK], F32, tag="sum", name="bias_sum")
+            nc.tensor.matmul(out=bias_sum[:], lhsT=ones[:], rhs=bias_rows[:, cols], start=True, stop=True)
+            nc.scalar.copy(out=bias_all[:, cols], in_=bias_sum[:])
 
         act_codes = const.tile([P, PASSES, B], U32, align_bytes=64)
         act_scales = const.tile([P, PASSES, B], U8, align_bytes=64)
@@ -81,6 +89,8 @@ def tile_lstmcell_pa_k_kernel(tc, x, me_output, W_memi, W_memh, W_memt, mem_bias
         x_slabs = []
         raw_tiles = []
         grouped_tiles = []
+        spread_banks = {}
+        quantised = {}
         turned = {}
         act_grouped = {}
         mg = [
@@ -88,18 +98,27 @@ def tile_lstmcell_pa_k_kernel(tc, x, me_output, W_memi, W_memh, W_memt, mem_bias
             for bt in range(B_TILES)
         ]
 
-        def load_activations(s):
+        def load_x(s, first, last):
+            if first == 0:
+                x_slabs.append(
+                    [
+                        slabs.tile([P, SLAB_PASSES * K_PASS], BF16, tag="slab%d" % bt, name="slab%d" % bt)
+                        for bt in range(B_TILES)
+                    ]
+                )
+            k0 = s * SLAB_PASSES * K_PASS
             for bt in range(B_TILES):
-                rows = slice(bt * P, (bt + 1) * P)
-                if s < X_SLABS:
-                    if bt == 0:
-                        x_slabs.append([])
-                    slab = slabs.tile([P, SLAB_PASSES * K_PASS], BF16, tag="slab%d" % bt, name="slab%d" % bt)
-                    width = SLAB_PASSES * K_PASS
-                    nc.sync.dma_start(out=slab[:], in_=x[rows, s * width : (s + 1) * width])
-                    x_slabs[s].append(slab)
-                else:
-                    nc.sync.dma_start(out=me_rows[bt][:], in_=me_output[rows, :])
+                nc.sync.dma_start(
+                    out=x_slabs[s][bt][:, first * K_PASS : last * K_PASS],
+                    in_=x[bt * P : (bt + 1) * P, k0 + first * K_PASS : k0 + last * K_PASS],
+                )
+
+        def load_activations(s):
+            if s < X_SLABS:
+                load_x(s, 0, SLAB_PASSES)
+            else:
+                for bt in range(B_TILES):
+                    nc.sync.dma_start(out=me_rows[bt][:], in_=me_output[bt * P : (bt + 1) * P, :])
 
         def load_raw(r):
             if r + SLAB_LEAD < PASSES and (r + SLAB_LEAD) % SLAB_PASSES == 0:
@@ -107,13 +126,17 @@ def tile_lstmcell_pa_k_kernel(tc, x, me_output, W_memi, W_memh, W_memt, mem_bias
             raw = raws.tile([P, BLOCKS_PER_RAW * PACK * N_BLOCK], BF16, tag="raw", name="raw")
             if r < X_PASSES:
                 rows_of_pass = W_memi[r * K_PASS : (r + 1) * K_PASS, :].rearrange("(q t) c -> q t c", t=PACK)
-                pieces = BLOCKS_PER_RAW if r == 0 else 1
-                width = OH // pieces
-                for piece in range(pieces):
-                    cols = slice(piece * width, (piece + 1) * width)
-                    nc.sync.dma_start(
-                        out=raw[:].rearrange("q (t c) -> q t c", t=PACK)[:, :, cols], in_=rows_of_pass[:, :, cols]
-                    )
+                if r < EARLY_TILES:
+                    for i in range(BLOCKS_PER_RAW):
+                        nc.sync.dma_start(
+                            out=raw[:].rearrange("q (i t c) -> q i t c", t=PACK, c=N_BLOCK)[:, i, :, :],
+                            in_=rows_of_pass[:, :, i * N_BLOCK : (i + 1) * N_BLOCK],
+                        )
+                        if r == 0 and i == 0:
+                            load_x(0, 0, 1)
+                    load_x(0, r + 1, r + 2 if r + 1 < EARLY_TILES else SLAB_PASSES)
+                else:
+                    nc.sync.dma_start(out=raw[:].rearrange("q (t c) -> q t c", t=PACK), in_=rows_of_pass)
             elif r < X_PASSES + COL_BLOCKS:
                 cb = r - X_PASSES
                 for g in range(ME_PASSES):
@@ -132,7 +155,7 @@ def tile_lstmcell_pa_k_kernel(tc, x, me_output, W_memi, W_memh, W_memt, mem_bias
             raw_tiles.append(raw)
 
         def block_source(r, i):
-            if r < X_PASSES:
+            if EARLY_TILES <= r < X_PASSES:
                 return raw_tiles[r][:].rearrange("q (t c) -> q t c", t=PACK)[:, :, i * N_BLOCK : (i + 1) * N_BLOCK]
             return raw_tiles[r][:].rearrange("p (g t c) -> p g t c", t=PACK, c=N_BLOCK)[:, i, :, :]
 
@@ -160,16 +183,34 @@ def tile_lstmcell_pa_k_kernel(tc, x, me_output, W_memi, W_memh, W_memt, mem_bias
                 in_=act_grouped[g][:].rearrange("p a b t -> p (a b t)"),
             )
 
+        def is_tensor_block(j):
+            return j % CYCLE == CYCLE - 1 and j < BLOCKS - 1
+
+        def spread(j, half):
+            source = block_source(j // BLOCKS_PER_RAW, j % BLOCKS_PER_RAW)
+            bank = spread_pool.tile([P, HALF, PACK], BF16, tag="spread", name="spread")
+            for part in range(2):
+                out_cols = slice(part * P, (part + 1) * P)
+                in_cols = slice(half * HALF + part * P, half * HALF + (part + 1) * P)
+                nc.tensor.matmul(
+                    out=bank[:, out_cols, :], lhsT=ident_bf16[:], rhs=source[:, :, in_cols].rearrange("q t c -> q c t"),
+                    start=True, stop=True,
+                )
+            spread_banks[(j, half)] = bank
+
         def regroup(j):
             source = block_source(j // BLOCKS_PER_RAW, j % BLOCKS_PER_RAW)
-            grouped = stream.tile([P, N_BLOCK, PACK], BF16, tag="grouped", name="grouped", bufs=8, align_bytes=64)
+            grouped = stream.tile([P, N_BLOCK, PACK], BF16, tag="grouped", name="grouped", bufs=9, align_bytes=64)
+            grouped_tiles.append(grouped)
+            if is_tensor_block(j):
+                nc.scalar.copy(out=grouped[:, 0:HALF, :], in_=spread_banks[(j, 0)][:])
+                return
             dst = grouped[:].rearrange("p (c i) t -> p c t i", i=4)
             src = source.rearrange("p t (c i) -> p c t i", i=4)
-            if j % 2 == 0:
-                nc.vector.tensor_copy(out=dst, in_=src)
-            else:
+            if j % CYCLE in (1, 3):
                 nc.scalar.copy(out=dst, in_=src)
-            grouped_tiles.append(grouped)
+            else:
+                nc.vector.tensor_copy(out=dst, in_=src)
 
         def multiply(sum_tiles, codes_of_pass, scales_of_pass, codes, scales, start, stop):
             for bt in range(B_TILES):
@@ -184,25 +225,31 @@ def tile_lstmcell_pa_k_kernel(tc, x, me_output, W_memi, W_memh, W_memt, mem_bias
                     stop=stop,
                 )
 
-        def finish(j):
+        def quantise_block(j):
             r, i = divmod(j, BLOCKS_PER_RAW)
             if r < X_PASSES + COL_BLOCKS:
-                codes = stream.tile([P, N_BLOCK], U32, tag="codes", name="codes", align_bytes=64)[:]
-                scales = stream.tile([P, N_BLOCK], U8, tag="scales", name="scales", align_bytes=64)[:]
+                codes_tile = stream.tile([P, N_BLOCK], U32, tag="codes", name="codes", align_bytes=64)
+                scales_tile = stream.tile([P, N_BLOCK], U8, tag="scales", name="scales", align_bytes=64)
+                codes, scales = codes_tile[:], scales_tile[:]
             else:
-                codes = read_codes[:, i, :]
-                scales = read_scales[:, i, :]
+                codes, scales = read_codes[:, i, :], read_scales[:, i, :]
             nc.vector.quantize_mx(
                 out=codes.bitcast(FP8X4), scales=scales, in_=grouped_tiles[j][:].rearrange("p c t -> p (c t)")
             )
-            if r < X_PASSES:
-                column = [mg[bt][i] for bt in range(B_TILES)]
-                multiply(column, act_codes[:, r, :], act_scales[:, r, :], codes, scales, r == 0, False)
-            elif r < X_PASSES + COL_BLOCKS:
-                cb = r - X_PASSES
-                g = X_PASSES + i
-                column = [mg[bt][cb] for bt in range(B_TILES)]
-                multiply(column, act_codes[:, g, :], act_scales[:, g, :], codes, scales, False, i == ME_PASSES - 1)
+            quantised[j] = (codes, scales)
+
+        def meets(j):
+            r, i = divmod(j, BLOCKS_PER_RAW)
+            return (r, i) if r < X_PASSES else (X_PASSES + i, r - X_PASSES)
+
+        def multiply_block(j):
+            g, cb = meets(j)
+            order = [b for b in product_order if meets(b)[1] == cb]
+            codes, scales = quantised[j]
+            multiply(
+                [mg[bt][cb] for bt in range(B_TILES)], act_codes[:, g, :], act_scales[:, g, :], codes, scales,
+                j == order[0], j == order[-1],
+            )
 
         z_tiles = {}
         gated_planes = {}
@@ -248,27 +295,46 @@ def tile_lstmcell_pa_k_kernel(tc, x, me_output, W_memi, W_memh, W_memt, mem_bias
 
         gate_stages = (add_bias, squash, mask_and_turn, collect, quantise_gated)
 
-        load_activations(0)
+        quantise_steps = [j + (SPREAD_LAG + 1 if is_tensor_block(j) else LAG) for j in range(BLOCKS)]
+        mg_blocks = (X_PASSES + COL_BLOCKS) * BLOCKS_PER_RAW
+        product_steps = [
+            quantise_steps[j] + (PRODUCT_LAG if j < BLOCKS - LAST_BLOCKS else 0) for j in range(mg_blocks)
+        ]
+        product_order = sorted(range(mg_blocks), key=lambda j: (product_steps[j], j))
+        done_steps = [max(product_steps[j] for j in range(mg_blocks) if meets(j)[1] == cb) for cb in range(COL_BLOCKS)]
+        collect_steps = [BLOCKS_PER_RAW * g for g in range(X_PASSES)]
+        collect_steps += [collect_steps[-1] + 2 * (g + 1) for g in range(ME_PASSES)]
+
         for r in range(LOAD_AHEAD):
             load_raw(r)
-        for step in range(-TURN_LEAD * BLOCKS_PER_RAW, BLOCKS + LAG + len(gate_stages)):
-            r, i = divmod(step, BLOCKS_PER_RAW)
-            if i == 0 and 0 <= r + COLLECT_LEAD < PASSES:
-                collect_activations(r + COLLECT_LEAD)
-            if i == 1 and 0 <= r + TURN_LEAD < PASSES:
-                turn_activations(r + TURN_LEAD)
+        for step in range(-TURN_LEAD, done_steps[-1] + len(gate_stages) + 1):
+            if step >= 0 and step % BLOCKS_PER_RAW == 0 and step // BLOCKS_PER_RAW + LOAD_AHEAD < RAW_TILES:
+                load_raw(step // BLOCKS_PER_RAW + LOAD_AHEAD)
+            if step + TURN_LEAD in collect_steps:
+                turn_activations(collect_steps.index(step + TURN_LEAD))
+            if 0 <= step + SPREAD_LEAD < BLOCKS and is_tensor_block(step + SPREAD_LEAD):
+                spread(step + SPREAD_LEAD, 0)
+            if step in collect_steps:
+                collect_activations(collect_steps.index(step))
             if 0 <= step < BLOCKS:
-                if i == 0 and r + LOAD_AHEAD < RAW_TILES:
-                    load_raw(r + LOAD_AHEAD)
                 regroup(step)
-            if i == 2 and 0 <= r + COLLECT_LEAD < PASSES:
-                quantise_activations(r + COLLECT_LEAD)
-            if LAG <= step < BLOCKS + LAG:
-                finish(step - LAG)
+                if is_tensor_block(step):
+                    spread(step, 1)
+            late = step - SPREAD_LAG
+            if 0 <= late < BLOCKS and is_tensor_block(late):
+                nc.vector.tensor_copy(out=grouped_tiles[late][:, HALF:, :], in_=spread_banks[(late, 1)][:])
+            if step - 1 in collect_steps:
+                quantise_activations(collect_steps.index(step - 1))
+            for j in range(BLOCKS):
+                if quantise_steps[j] == step:
+                    quantise_block(j)
+            for j in product_order:
+                if product_steps[j] == step:
+                    multiply_block(j)
             for n in range(len(gate_stages)):
-                cb, i_done = divmod(step - LAG - n - 1 - FIRST_MEMORY_BLOCK, BLOCKS_PER_RAW)
-                if 0 <= cb < COL_BLOCKS and i_done == BLOCKS_PER_RAW - 1:
-                    gate_stages[n](cb)
+                for cb in range(COL_BLOCKS):
+                    if done_steps[cb] + n + 1 == step:
+                        gate_stages[n](cb)
 
         out_sums = [sums.tile([P, H], F32, tag="sum", name="out_sum%d" % bt) for bt in range(B_TILES)]
         for g in range(ME_PASSES):

@@ -28,12 +28,11 @@ BLOCKS_PER_RAW = 3
 RAW_TILES = X_PASSES + COL_BLOCKS + 1
 BLOCKS = RAW_TILES * BLOCKS_PER_RAW
 
-SLAB_PASSES = 4
+SLAB_PASSES = 2
 X_SLABS = X_PASSES // SLAB_PASSES
 EARLY_TILES = 2
 LOAD_AHEAD = 5
 TURN_LEAD = 2
-SLAB_LEAD = 3
 CYCLE = 5
 HALF = N_BLOCK // 2
 SPREAD_LEAD = 1
@@ -121,8 +120,8 @@ def tile_lstmcell_pa_k_kernel(tc, x, me_output, W_memi, W_memh, W_memt, mem_bias
                     nc.sync.dma_start(out=me_rows[bt][:], in_=me_output[bt * P : (bt + 1) * P, :])
 
         def load_raw(r):
-            if r + SLAB_LEAD < PASSES and (r + SLAB_LEAD) % SLAB_PASSES == 0:
-                load_activations((r + SLAB_LEAD) // SLAB_PASSES)
+            if 0 < r <= X_PASSES and r % SLAB_PASSES == 0:
+                load_activations(r // SLAB_PASSES)
             raw = raws.tile([P, BLOCKS_PER_RAW * PACK * N_BLOCK], BF16, tag="raw", name="raw")
             if r < X_PASSES:
                 rows_of_pass = W_memi[r * K_PASS : (r + 1) * K_PASS, :].rearrange("(q t) c -> q t c", t=PACK)
@@ -134,7 +133,8 @@ def tile_lstmcell_pa_k_kernel(tc, x, me_output, W_memi, W_memh, W_memt, mem_bias
                         )
                         if r == 0 and i == 0:
                             load_x(0, 0, 1)
-                    load_x(0, r + 1, r + 2 if r + 1 < EARLY_TILES else SLAB_PASSES)
+                    if r == 0:
+                        load_x(0, 1, SLAB_PASSES)
                 else:
                     nc.sync.dma_start(out=raw[:].rearrange("q (t c) -> q t c", t=PACK), in_=rows_of_pass)
             elif r < X_PASSES + COL_BLOCKS:
@@ -193,7 +193,7 @@ def tile_lstmcell_pa_k_kernel(tc, x, me_output, W_memi, W_memh, W_memt, mem_bias
                 out_cols = slice(part * P, (part + 1) * P)
                 in_cols = slice(half * HALF + part * P, half * HALF + (part + 1) * P)
                 nc.tensor.matmul(
-                    out=bank[:, out_cols, :], lhsT=ident_bf16[:], rhs=source[:, :, in_cols].rearrange("q t c -> q c t"),
+                    out=bank[:, out_cols, :].rearrange("q c t -> q t c"), lhsT=ident_bf16[:], rhs=source[:, :, in_cols],
                     start=True, stop=True,
                 )
             spread_banks[(j, half)] = bank
@@ -207,7 +207,7 @@ def tile_lstmcell_pa_k_kernel(tc, x, me_output, W_memi, W_memh, W_memt, mem_bias
                 return
             dst = grouped[:].rearrange("p (c i) t -> p c t i", i=4)
             src = source.rearrange("p t (c i) -> p c t i", i=4)
-            if j % CYCLE in (1, 3):
+            if j % CYCLE in (1, 3) or j == 57:
                 nc.scalar.copy(out=dst, in_=src)
             else:
                 nc.vector.tensor_copy(out=dst, in_=src)

@@ -33,10 +33,6 @@ X_SLABS = X_PASSES // SLAB_PASSES
 EARLY_TILES = 2
 LOAD_AHEAD = 5
 TURN_LEAD = 2
-CYCLE = 5
-HALF = N_BLOCK // 2
-SPREAD_LEAD = 1
-SPREAD_LAG = 3
 LAG = 2
 PRODUCT_LAG = 3
 LAST_BLOCKS = 12
@@ -51,14 +47,11 @@ def tile_lstmcell_pa_k_kernel(tc, x, me_output, W_memi, W_memh, W_memt, mem_bias
         tc.tile_pool(name="stream", bufs=8) as stream,
         tc.tile_pool(name="gate", bufs=4) as gate_pool,
         tc.psum_pool(name="sums", bufs=B_TILES * COL_BLOCKS) as sums,
-        tc.psum_pool(name="turn", bufs=1) as turn,
-        tc.psum_pool(name="spread", bufs=1) as spread_pool,
+        tc.psum_pool(name="turn", bufs=2) as turn,
         tc.manual_schedule(),
     ):
         ident_f32 = const.tile([P, P], F32)
         make_identity(nc, ident_f32[:])
-        ident_bf16 = const.tile([P, P], BF16)
-        make_identity(nc, ident_bf16[:])
 
         warm = const.tile([P, 1], F32)
         nc.vector.memset(warm[:], 0.0)
@@ -88,7 +81,6 @@ def tile_lstmcell_pa_k_kernel(tc, x, me_output, W_memi, W_memh, W_memt, mem_bias
         x_slabs = []
         raw_tiles = []
         grouped_tiles = []
-        spread_banks = {}
         quantised = {}
         turned = {}
         act_grouped = {}
@@ -183,31 +175,13 @@ def tile_lstmcell_pa_k_kernel(tc, x, me_output, W_memi, W_memh, W_memt, mem_bias
                 in_=act_grouped[g][:].rearrange("p a b t -> p (a b t)"),
             )
 
-        def is_tensor_block(j):
-            return j % CYCLE == CYCLE - 1 and j < BLOCKS - 1
-
-        def spread(j, half):
-            source = block_source(j // BLOCKS_PER_RAW, j % BLOCKS_PER_RAW)
-            bank = spread_pool.tile([P, HALF, PACK], BF16, tag="spread", name="spread")
-            for part in range(2):
-                out_cols = slice(part * P, (part + 1) * P)
-                in_cols = slice(half * HALF + part * P, half * HALF + (part + 1) * P)
-                nc.tensor.matmul(
-                    out=bank[:, out_cols, :].rearrange("q c t -> q t c"), lhsT=ident_bf16[:], rhs=source[:, :, in_cols],
-                    start=True, stop=True,
-                )
-            spread_banks[(j, half)] = bank
-
         def regroup(j):
             source = block_source(j // BLOCKS_PER_RAW, j % BLOCKS_PER_RAW)
             grouped = stream.tile([P, N_BLOCK, PACK], BF16, tag="grouped", name="grouped", bufs=9, align_bytes=64)
             grouped_tiles.append(grouped)
-            if is_tensor_block(j):
-                nc.scalar.copy(out=grouped[:, 0:HALF, :], in_=spread_banks[(j, 0)][:])
-                return
             dst = grouped[:].rearrange("p (c i) t -> p c t i", i=4)
             src = source.rearrange("p t (c i) -> p c t i", i=4)
-            if j % CYCLE in (1, 3) or j == 57:
+            if j % 2 == 1:
                 nc.scalar.copy(out=dst, in_=src)
             else:
                 nc.vector.tensor_copy(out=dst, in_=src)
@@ -295,7 +269,19 @@ def tile_lstmcell_pa_k_kernel(tc, x, me_output, W_memi, W_memh, W_memt, mem_bias
 
         gate_stages = (add_bias, squash, mask_and_turn, collect, quantise_gated)
 
-        quantise_steps = [j + (SPREAD_LAG + 1 if is_tensor_block(j) else LAG) for j in range(BLOCKS)]
+        out_sums = []
+
+        def multiply_gated(g):
+            if g == 0:
+                for bt in range(B_TILES):
+                    out_sum = sums.tile([P, H], F32, tag="sum", name="out_sum%d" % bt)
+                    out_sums.append(out_sum)
+            multiply(
+                out_sums, gated_codes[:, g, :], gated_scales[:, g, :], read_codes[:, g, :], read_scales[:, g, :],
+                g == 0, g == ME_PASSES - 1,
+            )
+
+        quantise_steps = [j + LAG for j in range(BLOCKS)]
         mg_blocks = (X_PASSES + COL_BLOCKS) * BLOCKS_PER_RAW
         product_steps = [
             quantise_steps[j] + (PRODUCT_LAG if j < BLOCKS - LAST_BLOCKS else 0) for j in range(mg_blocks)
@@ -312,17 +298,10 @@ def tile_lstmcell_pa_k_kernel(tc, x, me_output, W_memi, W_memh, W_memt, mem_bias
                 load_raw(step // BLOCKS_PER_RAW + LOAD_AHEAD)
             if step + TURN_LEAD in collect_steps:
                 turn_activations(collect_steps.index(step + TURN_LEAD))
-            if 0 <= step + SPREAD_LEAD < BLOCKS and is_tensor_block(step + SPREAD_LEAD):
-                spread(step + SPREAD_LEAD, 0)
             if step in collect_steps:
                 collect_activations(collect_steps.index(step))
             if 0 <= step < BLOCKS:
                 regroup(step)
-                if is_tensor_block(step):
-                    spread(step, 1)
-            late = step - SPREAD_LAG
-            if 0 <= late < BLOCKS and is_tensor_block(late):
-                nc.vector.tensor_copy(out=grouped_tiles[late][:, HALF:, :], in_=spread_banks[(late, 1)][:])
             if step - 1 in collect_steps:
                 quantise_activations(collect_steps.index(step - 1))
             for j in range(BLOCKS):
@@ -335,13 +314,10 @@ def tile_lstmcell_pa_k_kernel(tc, x, me_output, W_memi, W_memh, W_memt, mem_bias
                 for cb in range(COL_BLOCKS):
                     if done_steps[cb] + n + 1 == step:
                         gate_stages[n](cb)
+            for g in range(ME_PASSES):
+                if max(done_steps[g] + len(gate_stages), quantise_steps[mg_blocks + g]) == step:
+                    multiply_gated(g)
 
-        out_sums = [sums.tile([P, H], F32, tag="sum", name="out_sum%d" % bt) for bt in range(B_TILES)]
-        for g in range(ME_PASSES):
-            multiply(
-                out_sums, gated_codes[:, g, :], gated_scales[:, g, :], read_codes[:, g, :], read_scales[:, g, :],
-                g == 0, g == ME_PASSES - 1,
-            )
         for bt in range(B_TILES):
             result = gate_pool.tile([P, H], F32, tag="result", name="result", bufs=2)
             if bt == 0:

@@ -33,6 +33,7 @@ X_SLABS = X_PASSES // SLAB_PASSES
 EARLY_TILES = 2
 LOAD_AHEAD = 5
 TURN_LEAD = 2
+RUN = 2
 LAG = 2
 PRODUCT_LAG = 3
 LAST_BLOCKS = 12
@@ -179,8 +180,8 @@ def tile_lstmcell_pa_k_kernel(tc, x, me_output, W_memi, W_memh, W_memt, mem_bias
             source = block_source(j // BLOCKS_PER_RAW, j % BLOCKS_PER_RAW)
             grouped = stream.tile([P, N_BLOCK, PACK], BF16, tag="grouped", name="grouped", bufs=9, align_bytes=64)
             grouped_tiles.append(grouped)
-            dst = grouped[:].rearrange("p (c i) t -> p c t i", i=4)
-            src = source.rearrange("p t (c i) -> p c t i", i=4)
+            dst = grouped[:].rearrange("p (c i) t -> p c t i", i=RUN)
+            src = source.rearrange("p t (c i) -> p c t i", i=RUN)
             if j % 2 == 1:
                 nc.scalar.copy(out=dst, in_=src)
             else:

@@ -33,7 +33,7 @@ X_SLABS = X_PASSES // SLAB_PASSES
 EARLY_TILES = 2
 LOAD_AHEAD = 5
 TURN_LEAD = 2
-RUN = 2
+RUN = 8
 LAG = 2
 PRODUCT_LAG = 3
 LAST_BLOCKS = 12

@@ -19,18 +19,20 @@ K_PASS = P * PACK
 N_BLOCK = 512
 B_TILES = B // P
 
-X_PASSES = I // K_PASS
 ME_PASSES = OH // K_PASS
-PASSES = X_PASSES + ME_PASSES
+X_PASSES = I // K_PASS
+PASSES = ME_PASSES + X_PASSES
 COL_BLOCKS = OH // N_BLOCK
 
 BLOCKS_PER_RAW = 3
-RAW_TILES = X_PASSES + COL_BLOCKS + 1
-BLOCKS = RAW_TILES * BLOCKS_PER_RAW
+MG_BLOCKS = PASSES * COL_BLOCKS
+BLOCKS = MG_BLOCKS + ME_PASSES
+RAW_TILES = BLOCKS // BLOCKS_PER_RAW
 
-SLAB_PASSES = 2
+SLAB_PASSES = 4
 X_SLABS = X_PASSES // SLAB_PASSES
-EARLY_TILES = 2
+EARLY_TILES = 0
+LAST_PASSES = 2
 LOAD_AHEAD = 5
 TURN_LEAD = 2
 RUN = 8
@@ -90,73 +92,70 @@ def tile_lstmcell_pa_k_kernel(tc, x, me_output, W_memi, W_memh, W_memt, mem_bias
             for bt in range(B_TILES)
         ]
 
-        def load_x(s, first, last):
-            if first == 0:
-                x_slabs.append(
-                    [
-                        slabs.tile([P, SLAB_PASSES * K_PASS], BF16, tag="slab%d" % bt, name="slab%d" % bt)
-                        for bt in range(B_TILES)
-                    ]
-                )
-            k0 = s * SLAB_PASSES * K_PASS
-            for bt in range(B_TILES):
-                nc.sync.dma_start(
-                    out=x_slabs[s][bt][:, first * K_PASS : last * K_PASS],
-                    in_=x[bt * P : (bt + 1) * P, k0 + first * K_PASS : k0 + last * K_PASS],
-                )
+        sequence = [(g, cb) for g in range(PASSES - LAST_PASSES) for cb in range(COL_BLOCKS)]
+        sequence += [(g, cb) for cb in range(COL_BLOCKS) for g in range(PASSES - LAST_PASSES, PASSES)]
 
-        def load_activations(s):
-            if s < X_SLABS:
-                load_x(s, 0, SLAB_PASSES)
+        def is_row_tile(r):
+            return EARLY_TILES <= r < PASSES - LAST_PASSES
+
+        def load_memory(first, last):
+            cols = slice(first * K_PASS, last * K_PASS)
+            for bt in range(B_TILES):
+                nc.sync.dma_start(out=me_rows[bt][:, cols], in_=me_output[bt * P : (bt + 1) * P, cols])
+
+        def load_x(s):
+            x_slabs.append([])
+            width = SLAB_PASSES * K_PASS
+            for bt in range(B_TILES):
+                slab = slabs.tile([P, width], BF16, tag="slab%d" % bt, name="slab%d" % bt)
+                nc.sync.dma_start(out=slab[:], in_=x[bt * P : (bt + 1) * P, s * width : (s + 1) * width])
+                x_slabs[s].append(slab)
+
+        def weight_rows(g):
+            if g < ME_PASSES:
+                rows = W_memh[g * K_PASS : (g + 1) * K_PASS, :]
             else:
-                for bt in range(B_TILES):
-                    nc.sync.dma_start(out=me_rows[bt][:], in_=me_output[bt * P : (bt + 1) * P, :])
+                rows = W_memi[(g - ME_PASSES) * K_PASS : (g - ME_PASSES + 1) * K_PASS, :]
+            return rows.rearrange("(q t) c -> q t c", t=PACK)
 
         def load_raw(r):
-            if 0 < r <= X_PASSES and r % SLAB_PASSES == 0:
-                load_activations(r // SLAB_PASSES)
+            if ME_PASSES <= r < PASSES and (r - ME_PASSES) % SLAB_PASSES == 0:
+                load_x((r - ME_PASSES) // SLAB_PASSES)
             raw = raws.tile([P, BLOCKS_PER_RAW * PACK * N_BLOCK], BF16, tag="raw", name="raw")
-            if r < X_PASSES:
-                rows_of_pass = W_memi[r * K_PASS : (r + 1) * K_PASS, :].rearrange("(q t) c -> q t c", t=PACK)
-                if r < EARLY_TILES:
-                    for i in range(BLOCKS_PER_RAW):
-                        nc.sync.dma_start(
-                            out=raw[:].rearrange("q (i t c) -> q i t c", t=PACK, c=N_BLOCK)[:, i, :, :],
-                            in_=rows_of_pass[:, :, i * N_BLOCK : (i + 1) * N_BLOCK],
-                        )
-                        if r == 0 and i == 0:
-                            load_x(0, 0, 1)
-                    if r == 0:
-                        load_x(0, 1, SLAB_PASSES)
-                else:
-                    nc.sync.dma_start(out=raw[:].rearrange("q (t c) -> q t c", t=PACK), in_=rows_of_pass)
-            elif r < X_PASSES + COL_BLOCKS:
-                cb = r - X_PASSES
-                for g in range(ME_PASSES):
-                    nc.sync.dma_start(
-                        out=raw[:].rearrange("q (g t c) -> q g t c", t=PACK, c=N_BLOCK)[:, g, :, :],
-                        in_=W_memh[g * K_PASS : (g + 1) * K_PASS, cb * N_BLOCK : (cb + 1) * N_BLOCK].rearrange(
-                            "(q t) c -> q t c", t=PACK
-                        ),
-                    )
-            else:
-                for g in range(ME_PASSES):
-                    nc.sync.dma_start(
-                        out=raw[:].rearrange("p (g t c) -> p g t c", t=PACK, c=N_BLOCK)[:, g, :, :],
-                        in_=W_memt[g * K_PASS : (g + 1) * K_PASS, :].rearrange("(p t) c -> p t c", t=PACK),
-                    )
             raw_tiles.append(raw)
+            if is_row_tile(r):
+                nc.sync.dma_start(out=raw[:].rearrange("q (t c) -> q t c", t=PACK), in_=weight_rows(r))
+                if r == 0:
+                    load_memory(0, ME_PASSES)
+                return
+            for i in range(BLOCKS_PER_RAW):
+                j = r * BLOCKS_PER_RAW + i
+                if j < MG_BLOCKS:
+                    g, cb = sequence[j]
+                    source = weight_rows(g)[:, :, cb * N_BLOCK : (cb + 1) * N_BLOCK]
+                else:
+                    g = j - MG_BLOCKS
+                    source = W_memt[g * K_PASS : (g + 1) * K_PASS, :].rearrange("(q t) c -> q t c", t=PACK)
+                nc.sync.dma_start(
+                    out=raw[:].rearrange("q (i t c) -> q i t c", t=PACK, c=N_BLOCK)[:, i, :, :], in_=source
+                )
+                if j == 0:
+                    load_memory(0, 1)
+            if r == 0:
+                load_memory(1, ME_PASSES)
 
-        def block_source(r, i):
-            if EARLY_TILES <= r < X_PASSES:
+        def block_source(j):
+            r, i = divmod(j, BLOCKS_PER_RAW)
+            if is_row_tile(r):
                 return raw_tiles[r][:].rearrange("q (t c) -> q t c", t=PACK)[:, :, i * N_BLOCK : (i + 1) * N_BLOCK]
-            return raw_tiles[r][:].rearrange("p (g t c) -> p g t c", t=PACK, c=N_BLOCK)[:, i, :, :]
+            return raw_tiles[r][:].rearrange("q (i t c) -> q i t c", t=PACK, c=N_BLOCK)[:, i, :, :]
 
         def turn_activations(g):
-            if g < X_PASSES:
-                row_tiles, local = x_slabs[g // SLAB_PASSES], g % SLAB_PASSES
+            if g < ME_PASSES:
+                row_tiles, local = me_rows, g
             else:
-                row_tiles, local = me_rows, g - X_PASSES
+                s, local = divmod(g - ME_PASSES, SLAB_PASSES)
+                row_tiles = x_slabs[s]
             words = turn.tile([P, B_TILES, 2, P], F32, tag="turn", name="words")
             for bt in range(B_TILES):
                 as_words = row_tiles[bt][:].bitcast(F32).rearrange("b (q u) -> b q u", u=2)
@@ -177,7 +176,7 @@ def tile_lstmcell_pa_k_kernel(tc, x, me_output, W_memi, W_memh, W_memt, mem_bias
             )
 
         def regroup(j):
-            source = block_source(j // BLOCKS_PER_RAW, j % BLOCKS_PER_RAW)
+            source = block_source(j)
             grouped = stream.tile([P, N_BLOCK, PACK], BF16, tag="grouped", name="grouped", bufs=9, align_bytes=64)
             grouped_tiles.append(grouped)
             dst = grouped[:].rearrange("p (c i) t -> p c t i", i=RUN)
@@ -201,29 +200,23 @@ def tile_lstmcell_pa_k_kernel(tc, x, me_output, W_memi, W_memh, W_memt, mem_bias
                 )
 
         def quantise_block(j):
-            r, i = divmod(j, BLOCKS_PER_RAW)
-            if r < X_PASSES + COL_BLOCKS:
+            if j < MG_BLOCKS:
                 codes_tile = stream.tile([P, N_BLOCK], U32, tag="codes", name="codes", align_bytes=64)
                 scales_tile = stream.tile([P, N_BLOCK], U8, tag="scales", name="scales", align_bytes=64)
                 codes, scales = codes_tile[:], scales_tile[:]
             else:
-                codes, scales = read_codes[:, i, :], read_scales[:, i, :]
+                codes, scales = read_codes[:, j - MG_BLOCKS, :], read_scales[:, j - MG_BLOCKS, :]
             nc.vector.quantize_mx(
                 out=codes.bitcast(FP8X4), scales=scales, in_=grouped_tiles[j][:].rearrange("p c t -> p (c t)")
             )
             quantised[j] = (codes, scales)
 
-        def meets(j):
-            r, i = divmod(j, BLOCKS_PER_RAW)
-            return (r, i) if r < X_PASSES else (X_PASSES + i, r - X_PASSES)
-
         def multiply_block(j):
-            g, cb = meets(j)
-            order = [b for b in product_order if meets(b)[1] == cb]
+            g, cb = sequence[j]
             codes, scales = quantised[j]
             multiply(
                 [mg[bt][cb] for bt in range(B_TILES)], act_codes[:, g, :], act_scales[:, g, :], codes, scales,
-                j == order[0], j == order[-1],
+                g == 0, g == PASSES - 1,
             )
 
         z_tiles = {}
@@ -282,15 +275,10 @@ def tile_lstmcell_pa_k_kernel(tc, x, me_output, W_memi, W_memh, W_memt, mem_bias
                 g == 0, g == ME_PASSES - 1,
             )
 
-        quantise_steps = [j + LAG for j in range(BLOCKS)]
-        mg_blocks = (X_PASSES + COL_BLOCKS) * BLOCKS_PER_RAW
-        product_steps = [
-            quantise_steps[j] + (PRODUCT_LAG if j < BLOCKS - LAST_BLOCKS else 0) for j in range(mg_blocks)
-        ]
-        product_order = sorted(range(mg_blocks), key=lambda j: (product_steps[j], j))
-        done_steps = [max(product_steps[j] for j in range(mg_blocks) if meets(j)[1] == cb) for cb in range(COL_BLOCKS)]
-        collect_steps = [BLOCKS_PER_RAW * g for g in range(X_PASSES)]
-        collect_steps += [collect_steps[-1] + 2 * (g + 1) for g in range(ME_PASSES)]
+        product_steps = [j + LAG + (PRODUCT_LAG if j < BLOCKS - LAST_BLOCKS else 0) for j in range(MG_BLOCKS)]
+        done_steps = [product_steps[sequence.index((PASSES - 1, cb))] for cb in range(COL_BLOCKS)]
+        collect_steps = [BLOCKS_PER_RAW * g for g in range(PASSES - LAST_PASSES)]
+        collect_steps += [collect_steps[-1] + 2 * (i + 1) for i in range(LAST_PASSES)]
 
         for r in range(LOAD_AHEAD):
             load_raw(r)
@@ -306,9 +294,9 @@ def tile_lstmcell_pa_k_kernel(tc, x, me_output, W_memi, W_memh, W_memt, mem_bias
             if step - 1 in collect_steps:
                 quantise_activations(collect_steps.index(step - 1))
             for j in range(BLOCKS):
-                if quantise_steps[j] == step:
+                if j + LAG == step:
                     quantise_block(j)
-            for j in product_order:
+            for j in range(MG_BLOCKS):
                 if product_steps[j] == step:
                     multiply_block(j)
             for n in range(len(gate_stages)):
@@ -316,7 +304,7 @@ def tile_lstmcell_pa_k_kernel(tc, x, me_output, W_memi, W_memh, W_memt, mem_bias
                     if done_steps[cb] + n + 1 == step:
                         gate_stages[n](cb)
             for g in range(ME_PASSES):
-                if max(done_steps[g] + len(gate_stages), quantise_steps[mg_blocks + g]) == step:
+                if max(done_steps[g] + len(gate_stages), MG_BLOCKS + g + LAG) == step:
                     multiply_gated(g)
 
         for bt in range(B_TILES):

@@ -38,6 +38,9 @@ TURN_LEAD = 2
 RUN = 8
 LAG = 2
 PRODUCT_LAG = 3
+MEMORY_LAG = 2
+SPLIT_BLOCKS = 6
+SPLIT_COLS = 192
 LAST_BLOCKS = 12
 
 
@@ -181,7 +184,11 @@ def tile_lstmcell_pa_k_kernel(tc, x, me_output, W_memi, W_memh, W_memt, mem_bias
             grouped_tiles.append(grouped)
             dst = grouped[:].rearrange("p (c i) t -> p c t i", i=RUN)
             src = source.rearrange("p t (c i) -> p c t i", i=RUN)
-            if j % 2 == 1:
+            if j >= BLOCKS - SPLIT_BLOCKS:
+                edge = SPLIT_COLS // RUN
+                nc.vector.tensor_copy(out=dst[:, :edge], in_=src[:, :edge])
+                nc.scalar.copy(out=dst[:, edge:], in_=src[:, edge:])
+            elif j % 2 == 1:
                 nc.scalar.copy(out=dst, in_=src)
             else:
                 nc.vector.tensor_copy(out=dst, in_=src)
@@ -277,8 +284,8 @@ def tile_lstmcell_pa_k_kernel(tc, x, me_output, W_memi, W_memh, W_memt, mem_bias
 
         product_steps = [j + LAG + (PRODUCT_LAG if j < BLOCKS - LAST_BLOCKS else 0) for j in range(MG_BLOCKS)]
         done_steps = [product_steps[sequence.index((PASSES - 1, cb))] for cb in range(COL_BLOCKS)]
-        collect_steps = [BLOCKS_PER_RAW * g for g in range(PASSES - LAST_PASSES)]
-        collect_steps += [collect_steps[-1] + 2 * (i + 1) for i in range(LAST_PASSES)]
+        collect_steps = [BLOCKS_PER_RAW * g + (MEMORY_LAG if g < ME_PASSES else 0) for g in range(PASSES - LAST_PASSES)]
+        collect_steps += [BLOCKS_PER_RAW * (PASSES - LAST_PASSES) - 1 + 2 * i for i in range(LAST_PASSES)]
 
         for r in range(LOAD_AHEAD):
             load_raw(r)

@@ -29,7 +29,7 @@ MG_BLOCKS = PASSES * COL_BLOCKS
 BLOCKS = MG_BLOCKS + ME_PASSES
 RAW_TILES = BLOCKS // BLOCKS_PER_RAW
 
-SLAB_PASSES = 4
+SLAB_PASSES = 2
 X_SLABS = X_PASSES // SLAB_PASSES
 EARLY_TILES = 0
 LAST_PASSES = 2
@@ -37,6 +37,7 @@ LOAD_AHEAD = 5
 TURN_LEAD = 2
 RUN = 8
 LAG = 2
+READ_LAG = 3
 PRODUCT_LAG = 3
 MEMORY_LAG = 2
 SPLIT_BLOCKS = 6
@@ -48,7 +49,7 @@ def tile_lstmcell_pa_k_kernel(tc, x, me_output, W_memi, W_memh, W_memt, mem_bias
     nc = tc.nc
     with (
         tc.tile_pool(name="const", bufs=1) as const,
-        tc.tile_pool(name="slabs", bufs=3) as slabs,
+        tc.tile_pool(name="slabs", bufs=6) as slabs,
         tc.tile_pool(name="raws", bufs=LOAD_AHEAD + 1) as raws,
         tc.tile_pool(name="stream", bufs=8) as stream,
         tc.tile_pool(name="gate", bufs=4) as gate_pool,
@@ -262,11 +263,13 @@ def tile_lstmcell_pa_k_kernel(tc, x, me_output, W_memi, W_memh, W_memt, mem_bias
             gated_grouped[cb] = grouped
 
         def quantise_gated(cb):
-            nc.vector.quantize_mx(
-                out=gated_codes[:, cb, :].bitcast(FP8X4),
-                scales=gated_scales[:, cb, :],
-                in_=gated_grouped[cb][:].rearrange("p a b t -> p (a b t)"),
-            )
+            for bt in range(B_TILES):
+                rows = slice(bt * P, (bt + 1) * P)
+                nc.vector.quantize_mx(
+                    out=gated_codes[:, cb, rows].bitcast(FP8X4),
+                    scales=gated_scales[:, cb, rows],
+                    in_=gated_grouped[cb][:, bt, :, :].rearrange("p b t -> p (b t)"),
+                )
 
         gate_stages = (add_bias, squash, mask_and_turn, collect, quantise_gated)
 
@@ -281,6 +284,9 @@ def tile_lstmcell_pa_k_kernel(tc, x, me_output, W_memi, W_memh, W_memt, mem_bias
                 out_sums, gated_codes[:, g, :], gated_scales[:, g, :], read_codes[:, g, :], read_scales[:, g, :],
                 g == 0, g == ME_PASSES - 1,
             )
+
+        def quantise_step(j):
+            return j + (LAG if j < MG_BLOCKS else READ_LAG)
 
         product_steps = [j + LAG + (PRODUCT_LAG if j < BLOCKS - LAST_BLOCKS else 0) for j in range(MG_BLOCKS)]
         done_steps = [product_steps[sequence.index((PASSES - 1, cb))] for cb in range(COL_BLOCKS)]
@@ -301,7 +307,7 @@ def tile_lstmcell_pa_k_kernel(tc, x, me_output, W_memi, W_memh, W_memt, mem_bias
             if step - 1 in collect_steps:
                 quantise_activations(collect_steps.index(step - 1))
             for j in range(BLOCKS):
-                if j + LAG == step:
+                if quantise_step(j) == step:
                     quantise_block(j)
             for j in range(MG_BLOCKS):
                 if product_steps[j] == step:
@@ -311,7 +317,7 @@ def tile_lstmcell_pa_k_kernel(tc, x, me_output, W_memi, W_memh, W_memt, mem_bias
                     if done_steps[cb] + n + 1 == step:
                         gate_stages[n](cb)
             for g in range(ME_PASSES):
-                if max(done_steps[g] + len(gate_stages), MG_BLOCKS + g + LAG) == step:
+                if max(done_steps[g] + len(gate_stages), quantise_step(MG_BLOCKS + g)) == step:
                     multiply_gated(g)
 
         for bt in range(B_TILES):

import concourse.mybir as mybir
from concourse.masks import make_identity

F32 = mybir.dt.float32
BF16 = mybir.dt.bfloat16
U32 = mybir.dt.uint32
U8 = mybir.dt.uint8
FP8X4 = mybir.dt.float8_e4m3fn_x4
ADD = mybir.AluOpType.add
MULT = mybir.AluOpType.mult
SIGMOID = mybir.ActivationFunctionType.Sigmoid

B, I, OH, H = 256, 8192, 1536, 512
FLOPS = 2 * B * (I * OH + OH * OH + OH * H)

P = 128
PACK = 4
K_PASS = P * PACK
N_BLOCK = 512
B_TILES = B // P

ME_PASSES = OH // K_PASS
X_PASSES = I // K_PASS
PASSES = ME_PASSES + X_PASSES
COL_BLOCKS = OH // N_BLOCK

BLOCKS_PER_RAW = 3
MG_BLOCKS = PASSES * COL_BLOCKS
BLOCKS = MG_BLOCKS + ME_PASSES
RAW_TILES = BLOCKS // BLOCKS_PER_RAW

SLAB_PASSES = 2
X_SLABS = X_PASSES // SLAB_PASSES
EARLY_TILES = 0
LAST_PASSES = 2
LOAD_AHEAD = 5
TURN_LEAD = 2
RUN = 8
LAG = 2
READ_LAG = 3
PRODUCT_LAG = 3
MEMORY_LAG = 2
SPLIT_BLOCKS = 6
SPLIT_COLS = 192
LAST_BLOCKS = 12


def tile_lstmcell_pa_k_kernel(tc, x, me_output, W_memi, W_memh, W_memt, mem_bias, out):
    nc = tc.nc
    with (
        tc.tile_pool(name="const", bufs=1) as const,
        tc.tile_pool(name="slabs", bufs=6) as slabs,
        tc.tile_pool(name="raws", bufs=LOAD_AHEAD + 1) as raws,
        tc.tile_pool(name="stream", bufs=8) as stream,
        tc.tile_pool(name="gate", bufs=4) as gate_pool,
        tc.psum_pool(name="sums", bufs=B_TILES * COL_BLOCKS) as sums,
        tc.psum_pool(name="turn", bufs=2) as turn,
        tc.manual_schedule(),
    ):
        ident_f32 = const.tile([P, P], F32)
        make_identity(nc, ident_f32[:])

        warm = const.tile([P, 1], F32)
        nc.vector.memset(warm[:], 0.0)
        nc.scalar.activation(out=warm[:], in_=warm[:], func=SIGMOID)

        bias_row = const.tile([1, OH], BF16)
        nc.sync.dma_start(out=bias_row[:], in_=mem_bias.rearrange("(o n) -> o n", o=1))
        ones = const.tile([P, P], BF16)
        nc.vector.memset(ones[:], 1.0)
        bias_rows = const.tile([P, OH], BF16)
        nc.gpsimd.memset(bias_rows[:].bitcast(F32), 0.0)
        nc.vector.tensor_copy(out=bias_rows[0:1, :], in_=bias_row[:])
        bias_all = const.tile([P, OH], BF16)
        for cb in range(COL_BLOCKS):
            cols = slice(cb * N_BLOCK, (cb + 1) * N_BLOCK)
            bias_sum = sums.tile([P, N_BLOCK], F32, tag="sum", name="bias_sum")
            nc.tensor.matmul(out=bias_sum[:], lhsT=ones[:], rhs=bias_rows[:, cols], start=True, stop=True)
            nc.scalar.copy(out=bias_all[:, cols], in_=bias_sum[:])

        act_codes = const.tile([P, PASSES, B], U32, align_bytes=64)
        act_scales = const.tile([P, PASSES, B], U8, align_bytes=64)
        gated_codes = const.tile([P, ME_PASSES, B], U32, align_bytes=64)
        gated_scales = const.tile([P, ME_PASSES, B], U8, align_bytes=64)
        read_codes = const.tile([P, ME_PASSES, H], U32, align_bytes=64)
        read_scales = const.tile([P, ME_PASSES, H], U8, align_bytes=64)
        me_rows = [const.tile([P, OH], BF16, name="me_rows%d" % bt) for bt in range(B_TILES)]
        x_slabs = []
        raw_tiles = []
        grouped_tiles = []
        quantised = {}
        turned = {}
        act_grouped = {}
        mg = [
            [sums.tile([P, N_BLOCK], F32, tag="sum", name="mg%d_%d" % (bt, cb)) for cb in range(COL_BLOCKS)]
            for bt in range(B_TILES)
        ]

        sequence = [(g, cb) for g in range(PASSES - LAST_PASSES) for cb in range(COL_BLOCKS)]
        sequence += [(g, cb) for cb in range(COL_BLOCKS) for g in range(PASSES - LAST_PASSES, PASSES)]

        def is_row_tile(r):
            return EARLY_TILES <= r < PASSES - LAST_PASSES

        def load_memory(first, last):
            cols = slice(first * K_PASS, last * K_PASS)
            for bt in range(B_TILES):
                nc.sync.dma_start(out=me_rows[bt][:, cols], in_=me_output[bt * P : (bt + 1) * P, cols])

        def load_x(s):
            x_slabs.append([])
            width = SLAB_PASSES * K_PASS
            for bt in range(B_TILES):
                slab = slabs.tile([P, width], BF16, tag="slab%d" % bt, name="slab%d" % bt)
                nc.sync.dma_start(out=slab[:], in_=x[bt * P : (bt + 1) * P, s * width : (s + 1) * width])
                x_slabs[s].append(slab)

        def weight_rows(g):
            if g < ME_PASSES:
                rows = W_memh[g * K_PASS : (g + 1) * K_PASS, :]
            else:
                rows = W_memi[(g - ME_PASSES) * K_PASS : (g - ME_PASSES + 1) * K_PASS, :]
            return rows.rearrange("(q t) c -> q t c", t=PACK)

        def load_raw(r):
            if ME_PASSES <= r < PASSES and (r - ME_PASSES) % SLAB_PASSES == 0:
                load_x((r - ME_PASSES) // SLAB_PASSES)
            raw = raws.tile([P, BLOCKS_PER_RAW * PACK * N_BLOCK], BF16, tag="raw", name="raw")
            raw_tiles.append(raw)
            if is_row_tile(r):
                nc.sync.dma_start(out=raw[:].rearrange("q (t c) -> q t c", t=PACK), in_=weight_rows(r))
                if r == 0:
                    load_memory(0, ME_PASSES)
                return
            for i in range(BLOCKS_PER_RAW):
                j = r * BLOCKS_PER_RAW + i
                if j < MG_BLOCKS:
                    g, cb = sequence[j]
                    source = weight_rows(g)[:, :, cb * N_BLOCK : (cb + 1) * N_BLOCK]
                else:
                    g = j - MG_BLOCKS
                    source = W_memt[g * K_PASS : (g + 1) * K_PASS, :].rearrange("(q t) c -> q t c", t=PACK)
                nc.sync.dma_start(
                    out=raw[:].rearrange("q (i t c) -> q i t c", t=PACK, c=N_BLOCK)[:, i, :, :], in_=source
                )
                if j == 0:
                    load_memory(0, 1)
            if r == 0:
                load_memory(1, ME_PASSES)

        def block_source(j):
            r, i = divmod(j, BLOCKS_PER_RAW)
            if is_row_tile(r):
                return raw_tiles[r][:].rearrange("q (t c) -> q t c", t=PACK)[:, :, i * N_BLOCK : (i + 1) * N_BLOCK]
            return raw_tiles[r][:].rearrange("q (i t c) -> q i t c", t=PACK, c=N_BLOCK)[:, i, :, :]

        def turn_activations(g):
            if g < ME_PASSES:
                row_tiles, local = me_rows, g
            else:
                s, local = divmod(g - ME_PASSES, SLAB_PASSES)
                row_tiles = x_slabs[s]
            words = turn.tile([P, B_TILES, 2, P], F32, tag="turn", name="words")
            for bt in range(B_TILES):
                as_words = row_tiles[bt][:].bitcast(F32).rearrange("b (q u) -> b q u", u=2)
                for u in range(2):
                    nc.tensor.transpose(words[:, bt, u, :], as_words[:, local * P : (local + 1) * P, u], ident_f32[:])
            turned[g] = words

        def collect_activations(g):
            grouped = stream.tile([P, B_TILES, P, PACK], BF16, tag="act_grouped", name="act_grouped", bufs=3, align_bytes=64)
            nc.scalar.copy(out=grouped[:].bitcast(F32), in_=turned[g][:].rearrange("q a u b -> q a b u"))
            act_grouped[g] = grouped

        def quantise_activations(g):
            nc.vector.quantize_mx(
                out=act_codes[:, g, :].bitcast(FP8X4),
                scales=act_scales[:, g, :],
                in_=act_grouped[g][:].rearrange("p a b t -> p (a b t)"),
            )

        def regroup(j):
            source = block_source(j)
            grouped = stream.tile([P, N_BLOCK, PACK], BF16, tag="grouped", name="grouped", bufs=9, align_bytes=64)
            grouped_tiles.append(grouped)
            dst = grouped[:].rearrange("p (c i) t -> p c t i", i=RUN)
            src = source.rearrange("p t (c i) -> p c t i", i=RUN)
            if j >= BLOCKS - SPLIT_BLOCKS:
                edge = SPLIT_COLS // RUN
                nc.vector.tensor_copy(out=dst[:, :edge], in_=src[:, :edge])
                nc.scalar.copy(out=dst[:, edge:], in_=src[:, edge:])
            elif j % 2 == 1:
                nc.scalar.copy(out=dst, in_=src)
            else:
                nc.vector.tensor_copy(out=dst, in_=src)

        def multiply(sum_tiles, codes_of_pass, scales_of_pass, codes, scales, start, stop):
            for bt in range(B_TILES):
                rows = slice(bt * P, (bt + 1) * P)
                nc.tensor.matmul_mx(
                    out=sum_tiles[bt][:],
                    lhsT=codes_of_pass[:, rows].bitcast(FP8X4),
                    lhsT_scale=scales_of_pass[:, rows],
                    rhs=codes.bitcast(FP8X4),
                    rhs_scale=scales,
                    start=start,
                    stop=stop,
                )

        def quantise_block(j):
            if j < MG_BLOCKS:
                codes_tile = stream.tile([P, N_BLOCK], U32, tag="codes", name="codes", align_bytes=64)
                scales_tile = stream.tile([P, N_BLOCK], U8, tag="scales", name="scales", align_bytes=64)
                codes, scales = codes_tile[:], scales_tile[:]
            else:
                codes, scales = read_codes[:, j - MG_BLOCKS, :], read_scales[:, j - MG_BLOCKS, :]
            nc.vector.quantize_mx(
                out=codes.bitcast(FP8X4), scales=scales, in_=grouped_tiles[j][:].rearrange("p c t -> p (c t)")
            )
            quantised[j] = (codes, scales)

        def multiply_block(j):
            g, cb = sequence[j]
            codes, scales = quantised[j]
            multiply(
                [mg[bt][cb] for bt in range(B_TILES)], act_codes[:, g, :], act_scales[:, g, :], codes, scales,
                g == 0, g == PASSES - 1,
            )

        z_tiles = {}
        gated_planes = {}
        gated_grouped = {}

        def add_bias(cb):
            cols = slice(cb * N_BLOCK, (cb + 1) * N_BLOCK)
            for bt in range(B_TILES):
                z = gate_pool.tile([P, N_BLOCK], F32, tag="z", name="z")
                nc.vector.tensor_tensor(out=z[:], in0=mg[bt][cb][:], in1=bias_all[:, cols], op=ADD)
                z_tiles[(cb, bt)] = z

        def squash(cb):
            for bt in range(B_TILES):
                z = z_tiles[(cb, bt)]
                nc.scalar.activation(out=z[:], in_=z[:], func=SIGMOID)

        def mask_and_turn(cb):
            cols = slice(cb * N_BLOCK, (cb + 1) * N_BLOCK)
            for bt in range(B_TILES):
                gated = gate_pool.tile([P, N_BLOCK], BF16, tag="gated", name="gated")
                nc.vector.tensor_tensor(out=gated[:], in0=z_tiles[(cb, bt)][:], in1=me_rows[bt][:, cols], op=MULT)
                words = turn.tile([P, 2, P], F32, tag="turn", name="gated_words")
                as_words = gated[:].bitcast(F32).rearrange("b (q u) -> b q u", u=2)
                for u in range(2):
                    nc.tensor.transpose(words[:, u, :], as_words[:, :, u], ident_f32[:])
                gated_planes[(cb, bt)] = words

        def collect(cb):
            grouped = gate_pool.tile([P, B_TILES, P, PACK], BF16, tag="gated_grouped", name="gated_grouped", bufs=2, align_bytes=64)
            for bt in range(B_TILES):
                nc.scalar.copy(
                    out=grouped[:].bitcast(F32)[:, bt, :, :], in_=gated_planes[(cb, bt)][:].rearrange("q u b -> q b u")
                )
            gated_grouped[cb] = grouped

        def quantise_gated(cb):
            for bt in range(B_TILES):
                rows = slice(bt * P, (bt + 1) * P)
                nc.vector.quantize_mx(
                    out=gated_codes[:, cb, rows].bitcast(FP8X4),
                    scales=gated_scales[:, cb, rows],
                    in_=gated_grouped[cb][:, bt, :, :].rearrange("p b t -> p (b t)"),
                )

        gate_stages = (add_bias, squash, mask_and_turn, collect, quantise_gated)

        out_sums = []

        def multiply_gated(g):
            if g == 0:
                for bt in range(B_TILES):
                    out_sum = sums.tile([P, H], F32, tag="sum", name="out_sum%d" % bt)
                    out_sums.append(out_sum)
            multiply(
                out_sums, gated_codes[:, g, :], gated_scales[:, g, :], read_codes[:, g, :], read_scales[:, g, :],
                g == 0, g == ME_PASSES - 1,
            )

        def quantise_step(j):
            return j + (LAG if j < MG_BLOCKS else READ_LAG)

        product_steps = [j + LAG + (PRODUCT_LAG if j < BLOCKS - LAST_BLOCKS else 0) for j in range(MG_BLOCKS)]
        done_steps = [product_steps[sequence.index((PASSES - 1, cb))] for cb in range(COL_BLOCKS)]
        collect_steps = [BLOCKS_PER_RAW * g + (MEMORY_LAG if g < ME_PASSES else 0) for g in range(PASSES - LAST_PASSES)]
        collect_steps += [BLOCKS_PER_RAW * (PASSES - LAST_PASSES) - 1 + 2 * i for i in range(LAST_PASSES)]

        for r in range(LOAD_AHEAD):
            load_raw(r)
        for step in range(-TURN_LEAD, done_steps[-1] + len(gate_stages) + 1):
            if step >= 0 and step % BLOCKS_PER_RAW == 0 and step // BLOCKS_PER_RAW + LOAD_AHEAD < RAW_TILES:
                load_raw(step // BLOCKS_PER_RAW + LOAD_AHEAD)
            if step + TURN_LEAD in collect_steps:
                turn_activations(collect_steps.index(step + TURN_LEAD))
            if step in collect_steps:
                collect_activations(collect_steps.index(step))
            if 0 <= step < BLOCKS:
                regroup(step)
            if step - 1 in collect_steps:
                quantise_activations(collect_steps.index(step - 1))
            for j in range(BLOCKS):
                if quantise_step(j) == step:
                    quantise_block(j)
            for j in range(MG_BLOCKS):
                if product_steps[j] == step:
                    multiply_block(j)
            for n in range(len(gate_stages)):
                for cb in range(COL_BLOCKS):
                    if done_steps[cb] + n + 1 == step:
                        gate_stages[n](cb)
            for g in range(ME_PASSES):
                if max(done_steps[g] + len(gate_stages), quantise_step(MG_BLOCKS + g)) == step:
                    multiply_gated(g)

        for bt in range(B_TILES):
            result = gate_pool.tile([P, H], F32, tag="result", name="result", bufs=2)
            if bt == 0:
                nc.scalar.copy(out=result[:], in_=out_sums[bt][:])
            else:
                nc.vector.tensor_copy(out=result[:], in_=out_sums[bt][:])
            nc.sync.dma_start(out=out[bt * P : (bt + 1) * P, :], in_=result[:])
